import numpy as np
import ml_dtypes

BF16 = ml_dtypes.bfloat16


def bf(x):
    return np.asarray(x, np.float32).astype(BF16)


def f32(x):
    return np.asarray(x, np.float32)


def f64(x):
    return np.asarray(x).astype(np.float64)


def striped(idx):
    return np.tile(idx.reshape(-1, 16).T, (8, 1))


H, S, N, M = 128, 512, 128, 256


def sigmoid(v):
    return 1.0 / (1.0 + np.exp(-v))


def setup_inputs():
    return {
        "table": bf(np.random.standard_normal((S, H))),
        "prev": bf(np.random.standard_normal((H, N))),
        "wm": bf(np.random.standard_normal((H, H)) / np.sqrt(H)),
        "bm": f32(0.1 * np.random.standard_normal((H, 1))),
        "mem_gate": f32(0.5 * np.random.standard_normal((H, 1))),
        "wq": bf(np.random.standard_normal((H, H)) / np.sqrt(H)),
        "bq": f32(0.1 * np.random.standard_normal((H, 1))),
        "offs": striped(np.random.permutation(np.tile(np.arange(S), 2))[:N]),
    }


def reference(table, prev, wm, bm, mem_gate, wq, bq, offs):
    idx = offs[:16].T.reshape(-1)
    gate = sigmoid(f64(mem_gate))
    ts = f64(table).T * (1.0 - gate)
    memg = np.tanh(f64(wm).T @ f64(prev) + f64(bm)) * gate
    h0 = ts[:, idx] + memg
    q = f64(wq).T @ ts[:, idx] + f64(wq).T @ memg + f64(bq)
    res = np.empty((M, N), np.float64)
    res[:H] = h0
    res[H:] = q
    return res

@@ -1,0 +1,75 @@
+import concourse.mybir as mybir
+from concourse.masks import make_identity
+
+P = 128
+S = 512
+N = 128
+BLOCKS = S // P
+
+BF16, F32, U16 = mybir.dt.bfloat16, mybir.dt.float32, mybir.dt.uint16
+ACT = mybir.ActivationFunctionType
+ALU = mybir.AluOpType
+
+FLOPS = 3 * 2 * P * P * N
+
+
+def tile_socialtnn_kernel(tc, table, prev, wm, bm, mem_gate, wq, bq, offs, out):
+    nc = tc.nc
+    with (
+        tc.tile_pool(name="held", bufs=1) as held,
+        tc.psum_pool(name="psum", bufs=1) as psum,
+    ):
+        offsets = held.tile([P, N // 16], U16, name="offsets")
+        nc.sync.dma_start(offsets[:], offs)
+
+        mem_gate_sb = held.tile([P, 1], F32, name="mem_gate_sb")
+        nc.sync.dma_start(mem_gate_sb[:], mem_gate)
+        table_sb = held.tile([P, BLOCKS, P], BF16, name="table_sb")
+        nc.sync.dma_start(table_sb[:], table.rearrange("(b p) h -> p b h", p=P))
+
+        wm_sb = held.tile([P, P], BF16, name="wm_sb")
+        nc.scalar.dma_start(wm_sb[:], wm)
+        prev_sb = held.tile([P, N], BF16, name="prev_sb")
+        nc.scalar.dma_start(prev_sb[:], prev)
+        bm_sb = held.tile([P, 1], F32, name="bm_sb")
+        nc.scalar.dma_start(bm_sb[:], bm)
+
+        identity = held.tile([P, P], BF16, name="identity")
+        make_identity(nc, identity[:])
+        wq_sb = held.tile([P, P], BF16, name="wq_sb")
+        nc.gpsimd.dma_start(wq_sb[:], wq)
+        bq_sb = held.tile([P, 1], F32, name="bq_sb")
+        nc.gpsimd.dma_start(bq_sb[:], bq)
+
+        one_minus_gate = held.tile([P, 1], F32, name="one_minus_gate")
+        nc.scalar.activation(one_minus_gate[:], mem_gate_sb[:], ACT.Sigmoid, scale=-1.0)
+        gate = held.tile([P, 1], F32, name="gate")
+        nc.scalar.activation(gate[:], mem_gate_sb[:], ACT.Sigmoid)
+
+        table_t_ps = psum.tile([P, S], BF16, name="table_t_ps")
+        for b in range(BLOCKS):
+            nc.tensor.transpose(table_t_ps[:, b * P : (b + 1) * P], table_sb[:, b, :], identity[:])
+        ts = held.tile([P, S], BF16, name="ts")
+        nc.vector.tensor_scalar_mul(ts[:], table_t_ps[:], one_minus_gate[:, 0:1])
+
+        pre_ps = psum.tile([P, N], F32, name="pre_ps")
+        nc.tensor.matmul(pre_ps[:], wm_sb[:], prev_sb[:], start=True, stop=True)
+        tanh_sb = held.tile([P, N], F32, name="tanh_sb")
+        nc.scalar.activation(tanh_sb[:], pre_ps[:], ACT.Tanh, bias=bm_sb[:, 0:1])
+        memg_bf = held.tile([P, N], BF16, name="memg_bf")
+        nc.vector.tensor_scalar_mul(memg_bf[:], tanh_sb[:], gate[:, 0:1])
+
+        picked_ps = psum.tile([P, N], F32, name="picked_ps")
+        nc.tensor.matmul(picked_ps[:], identity[:], ts[:].indirect(offsets[:]), start=True, stop=True)
+        q_ps = psum.tile([P, N], F32, name="q_ps")
+        nc.tensor.matmul(q_ps[:], wq_sb[:], ts[:].indirect(offsets[:]), start=True, stop=False)
+        nc.tensor.matmul(q_ps[:], wq_sb[:], memg_bf[:], start=False, stop=True)
+
+        h0_sb = held.tile([P, N], F32, name="h0_sb")
+        nc.vector.scalar_tensor_tensor(
+            h0_sb[:], tanh_sb[:], gate[:, 0:1], picked_ps[:], op0=ALU.mult, op1=ALU.add
+        )
+        nc.sync.dma_start(out[0:P, :], h0_sb[:])
+        q_sb = held.tile([P, N], F32, name="q_sb")
+        nc.scalar.activation(q_sb[:], q_ps[:], ACT.Identity, bias=bq_sb[:, 0:1])
+        nc.scalar.dma_start(out[P : 2 * P, :], q_sb[:])

@@ -19,14 +19,17 @@ def tile_socialtnn_kernel(tc, table, prev, wm, bm, mem_gate, wq, bq, offs, out):
         tc.tile_pool(name="held", bufs=1) as held,
         tc.psum_pool(name="psum", bufs=1) as psum,
     ):
-        offsets = held.tile([P, N // 16], U16, name="offsets")
-        nc.sync.dma_start(offsets[:], offs)
-
-        mem_gate_sb = held.tile([P, 1], F32, name="mem_gate_sb")
-        nc.sync.dma_start(mem_gate_sb[:], mem_gate)
         table_sb = held.tile([P, BLOCKS, P], BF16, name="table_sb")
         nc.sync.dma_start(table_sb[:], table.rearrange("(b p) h -> p b h", p=P))
+        offsets = held.tile([P, N // 16], U16, name="offsets")
+        nc.sync.dma_start(offsets[:], offs)
+        wq_sb = held.tile([P, P], BF16, name="wq_sb")
+        nc.sync.dma_start(wq_sb[:], wq)
+        bq_sb = held.tile([P, 1], F32, name="bq_sb")
+        nc.sync.dma_start(bq_sb[:], bq)
 
+        mem_gate_sb = held.tile([P, 1], F32, name="mem_gate_sb")
+        nc.scalar.dma_start(mem_gate_sb[:], mem_gate)
         wm_sb = held.tile([P, P], BF16, name="wm_sb")
         nc.scalar.dma_start(wm_sb[:], wm)
         prev_sb = held.tile([P, N], BF16, name="prev_sb")
@@ -36,21 +39,11 @@ def tile_socialtnn_kernel(tc, table, prev, wm, bm, mem_gate, wq, bq, offs, out):
 
         identity = held.tile([P, P], BF16, name="identity")
         make_identity(nc, identity[:])
-        wq_sb = held.tile([P, P], BF16, name="wq_sb")
-        nc.gpsimd.dma_start(wq_sb[:], wq)
-        bq_sb = held.tile([P, 1], F32, name="bq_sb")
-        nc.gpsimd.dma_start(bq_sb[:], bq)
 
         one_minus_gate = held.tile([P, 1], F32, name="one_minus_gate")
         nc.scalar.activation(one_minus_gate[:], mem_gate_sb[:], ACT.Sigmoid, scale=-1.0)
         gate = held.tile([P, 1], F32, name="gate")
         nc.scalar.activation(gate[:], mem_gate_sb[:], ACT.Sigmoid)
-
-        table_t_ps = psum.tile([P, S], BF16, name="table_t_ps")
-        for b in range(BLOCKS):
-            nc.tensor.transpose(table_t_ps[:, b * P : (b + 1) * P], table_sb[:, b, :], identity[:])
-        ts = held.tile([P, S], BF16, name="ts")
-        nc.vector.tensor_scalar_mul(ts[:], table_t_ps[:], one_minus_gate[:, 0:1])
 
         pre_ps = psum.tile([P, N], F32, name="pre_ps")
         nc.tensor.matmul(pre_ps[:], wm_sb[:], prev_sb[:], start=True, stop=True)
@@ -59,11 +52,17 @@ def tile_socialtnn_kernel(tc, table, prev, wm, bm, mem_gate, wq, bq, offs, out):
         memg_bf = held.tile([P, N], BF16, name="memg_bf")
         nc.vector.tensor_scalar_mul(memg_bf[:], tanh_sb[:], gate[:, 0:1])
 
+        table_t_ps = psum.tile([P, S], BF16, name="table_t_ps")
+        for b in range(BLOCKS):
+            nc.tensor.transpose(table_t_ps[:, b * P : (b + 1) * P], table_sb[:, b, :], identity[:])
+        ts = held.tile([P, S], BF16, name="ts")
+        nc.vector.tensor_scalar_mul(ts[:], table_t_ps[:], one_minus_gate[:, 0:1])
+
+        q_ps = psum.tile([P, N], F32, name="q_ps")
+        nc.tensor.matmul(q_ps[:], wq_sb[:], memg_bf[:], start=True, stop=False)
+        nc.tensor.matmul(q_ps[:], wq_sb[:], ts[:].indirect(offsets[:]), start=False, stop=True)
         picked_ps = psum.tile([P, N], F32, name="picked_ps")
         nc.tensor.matmul(picked_ps[:], identity[:], ts[:].indirect(offsets[:]), start=True, stop=True)
-        q_ps = psum.tile([P, N], F32, name="q_ps")
-        nc.tensor.matmul(q_ps[:], wq_sb[:], ts[:].indirect(offsets[:]), start=True, stop=False)
-        nc.tensor.matmul(q_ps[:], wq_sb[:], memg_bf[:], start=False, stop=True)
 
         h0_sb = held.tile([P, N], F32, name="h0_sb")
         nc.vector.scalar_tensor_tensor(

@@ -21,21 +21,21 @@ def tile_socialtnn_kernel(tc, table, prev, wm, bm, mem_gate, wq, bq, offs, out):
     ):
         table_sb = held.tile([P, BLOCKS, P], BF16, name="table_sb")
         nc.sync.dma_start(table_sb[:], table.rearrange("(b p) h -> p b h", p=P))
+        mem_gate_sb = held.tile([P, 1], F32, name="mem_gate_sb")
+        nc.sync.dma_start(mem_gate_sb[:], mem_gate)
         offsets = held.tile([P, N // 16], U16, name="offsets")
         nc.sync.dma_start(offsets[:], offs)
-        wq_sb = held.tile([P, P], BF16, name="wq_sb")
-        nc.sync.dma_start(wq_sb[:], wq)
         bq_sb = held.tile([P, 1], F32, name="bq_sb")
         nc.sync.dma_start(bq_sb[:], bq)
 
-        mem_gate_sb = held.tile([P, 1], F32, name="mem_gate_sb")
-        nc.scalar.dma_start(mem_gate_sb[:], mem_gate)
         wm_sb = held.tile([P, P], BF16, name="wm_sb")
         nc.scalar.dma_start(wm_sb[:], wm)
         prev_sb = held.tile([P, N], BF16, name="prev_sb")
         nc.scalar.dma_start(prev_sb[:], prev)
         bm_sb = held.tile([P, 1], F32, name="bm_sb")
         nc.scalar.dma_start(bm_sb[:], bm)
+        wq_sb = held.tile([P, P], BF16, name="wq_sb")
+        nc.scalar.dma_start(wq_sb[:], wq)
 
         identity = held.tile([P, P], BF16, name="identity")
         make_identity(nc, identity[:])
@@ -45,6 +45,12 @@ def tile_socialtnn_kernel(tc, table, prev, wm, bm, mem_gate, wq, bq, offs, out):
         gate = held.tile([P, 1], F32, name="gate")
         nc.scalar.activation(gate[:], mem_gate_sb[:], ACT.Sigmoid)
 
+        table_t_ps = psum.tile([P, S], BF16, name="table_t_ps")
+        for b in range(BLOCKS):
+            nc.tensor.transpose(table_t_ps[:, b * P : (b + 1) * P], table_sb[:, b, :], identity[:])
+        ts = held.tile([P, S], BF16, name="ts")
+        nc.vector.tensor_scalar_mul(ts[:], table_t_ps[:], one_minus_gate[:, 0:1])
+
         pre_ps = psum.tile([P, N], F32, name="pre_ps")
         nc.tensor.matmul(pre_ps[:], wm_sb[:], prev_sb[:], start=True, stop=True)
         tanh_sb = held.tile([P, N], F32, name="tanh_sb")
@@ -52,17 +58,11 @@ def tile_socialtnn_kernel(tc, table, prev, wm, bm, mem_gate, wq, bq, offs, out):
         memg_bf = held.tile([P, N], BF16, name="memg_bf")
         nc.vector.tensor_scalar_mul(memg_bf[:], tanh_sb[:], gate[:, 0:1])
 
-        table_t_ps = psum.tile([P, S], BF16, name="table_t_ps")
-        for b in range(BLOCKS):
-            nc.tensor.transpose(table_t_ps[:, b * P : (b + 1) * P], table_sb[:, b, :], identity[:])
-        ts = held.tile([P, S], BF16, name="ts")
-        nc.vector.tensor_scalar_mul(ts[:], table_t_ps[:], one_minus_gate[:, 0:1])
-
-        q_ps = psum.tile([P, N], F32, name="q_ps")
-        nc.tensor.matmul(q_ps[:], wq_sb[:], memg_bf[:], start=True, stop=False)
-        nc.tensor.matmul(q_ps[:], wq_sb[:], ts[:].indirect(offsets[:]), start=False, stop=True)
         picked_ps = psum.tile([P, N], F32, name="picked_ps")
         nc.tensor.matmul(picked_ps[:], identity[:], ts[:].indirect(offsets[:]), start=True, stop=True)
+        q_ps = psum.tile([P, N], F32, name="q_ps")
+        nc.tensor.matmul(q_ps[:], wq_sb[:], ts[:].indirect(offsets[:]), start=True, stop=False)
+        nc.tensor.matmul(q_ps[:], wq_sb[:], memg_bf[:], start=False, stop=True)
 
         h0_sb = held.tile([P, N], F32, name="h0_sb")
         nc.vector.scalar_tensor_tensor(

@@ -5,10 +5,13 @@ P = 128
 S = 512
 N = 128
 BLOCKS = S // P
+HALF_BLOCKS = BLOCKS // 2
 
 BF16, F32, U16 = mybir.dt.bfloat16, mybir.dt.float32, mybir.dt.uint16
 ACT = mybir.ActivationFunctionType
 ALU = mybir.AluOpType
+
+WARM_MATMULS = 4
 
 FLOPS = 3 * 2 * P * P * N
 
@@ -19,37 +22,51 @@ def tile_socialtnn_kernel(tc, table, prev, wm, bm, mem_gate, wq, bq, offs, out):
         tc.tile_pool(name="held", bufs=1) as held,
         tc.psum_pool(name="psum", bufs=1) as psum,
     ):
+        wm_sb = held.tile([P, P], BF16, name="wm_sb")
+        nc.sync.dma_start(wm_sb[:], wm)
+        prev_sb = held.tile([P, N], BF16, name="prev_sb")
+        nc.sync.dma_start(prev_sb[:], prev)
         table_sb = held.tile([P, BLOCKS, P], BF16, name="table_sb")
-        nc.sync.dma_start(table_sb[:], table.rearrange("(b p) h -> p b h", p=P))
-        mem_gate_sb = held.tile([P, 1], F32, name="mem_gate_sb")
-        nc.sync.dma_start(mem_gate_sb[:], mem_gate)
+        table_blocks = table.rearrange("(b p) h -> p b h", p=P)
+        for half in range(2):
+            blocks = slice(half * HALF_BLOCKS, (half + 1) * HALF_BLOCKS)
+            nc.sync.dma_start(table_sb[:, blocks, :], table_blocks[:, blocks, :])
         offsets = held.tile([P, N // 16], U16, name="offsets")
         nc.sync.dma_start(offsets[:], offs)
-        bq_sb = held.tile([P, 1], F32, name="bq_sb")
-        nc.sync.dma_start(bq_sb[:], bq)
 
-        wm_sb = held.tile([P, P], BF16, name="wm_sb")
-        nc.scalar.dma_start(wm_sb[:], wm)
-        prev_sb = held.tile([P, N], BF16, name="prev_sb")
-        nc.scalar.dma_start(prev_sb[:], prev)
+        mem_gate_sb = held.tile([P, 1], F32, name="mem_gate_sb")
+        nc.scalar.dma_start(mem_gate_sb[:], mem_gate)
         bm_sb = held.tile([P, 1], F32, name="bm_sb")
         nc.scalar.dma_start(bm_sb[:], bm)
-        wq_sb = held.tile([P, P], BF16, name="wq_sb")
-        nc.scalar.dma_start(wq_sb[:], wq)
 
         identity = held.tile([P, P], BF16, name="identity")
         make_identity(nc, identity[:])
+        wq_sb = held.tile([P, P], BF16, name="wq_sb")
+        nc.gpsimd.dma_start(wq_sb[:], wq)
+        bq_sb = held.tile([P, 1], F32, name="bq_sb")
+        nc.gpsimd.dma_start(bq_sb[:], bq)
+
+        zeros = held.tile([P, S], BF16, name="zeros")
+        nc.vector.memset(zeros[:], 0.0)
+        warm_ps = psum.tile([P, S], F32, name="warm_ps")
+        for i in range(WARM_MATMULS):
+            nc.tensor.matmul(warm_ps[:], zeros[:, 0:P], zeros[:], start=True, stop=True)
 
         one_minus_gate = held.tile([P, 1], F32, name="one_minus_gate")
         nc.scalar.activation(one_minus_gate[:], mem_gate_sb[:], ACT.Sigmoid, scale=-1.0)
         gate = held.tile([P, 1], F32, name="gate")
         nc.scalar.activation(gate[:], mem_gate_sb[:], ACT.Sigmoid)
 
-        table_t_ps = psum.tile([P, S], BF16, name="table_t_ps")
-        for b in range(BLOCKS):
-            nc.tensor.transpose(table_t_ps[:, b * P : (b + 1) * P], table_sb[:, b, :], identity[:])
         ts = held.tile([P, S], BF16, name="ts")
-        nc.vector.tensor_scalar_mul(ts[:], table_t_ps[:], one_minus_gate[:, 0:1])
+        for half in range(2):
+            table_t_ps = psum.tile([P, S // 2], BF16, name=f"table_t_ps{half}")
+            for i in range(HALF_BLOCKS):
+                nc.tensor.transpose(
+                    table_t_ps[:, i * P : (i + 1) * P], table_sb[:, half * HALF_BLOCKS + i, :], identity[:]
+                )
+            nc.vector.tensor_scalar_mul(
+                ts[:, half * (S // 2) : (half + 1) * (S // 2)], table_t_ps[:], one_minus_gate[:, 0:1]
+            )
 
         pre_ps = psum.tile([P, N], F32, name="pre_ps")
         nc.tensor.matmul(pre_ps[:], wm_sb[:], prev_sb[:], start=True, stop=True)

@@ -22,20 +22,18 @@ def tile_socialtnn_kernel(tc, table, prev, wm, bm, mem_gate, wq, bq, offs, out):
         tc.tile_pool(name="held", bufs=1) as held,
         tc.psum_pool(name="psum", bufs=1) as psum,
     ):
-        wm_sb = held.tile([P, P], BF16, name="wm_sb")
-        nc.sync.dma_start(wm_sb[:], wm)
-        prev_sb = held.tile([P, N], BF16, name="prev_sb")
-        nc.sync.dma_start(prev_sb[:], prev)
-        table_sb = held.tile([P, BLOCKS, P], BF16, name="table_sb")
-        table_blocks = table.rearrange("(b p) h -> p b h", p=P)
-        for half in range(2):
-            blocks = slice(half * HALF_BLOCKS, (half + 1) * HALF_BLOCKS)
-            nc.sync.dma_start(table_sb[:, blocks, :], table_blocks[:, blocks, :])
         offsets = held.tile([P, N // 16], U16, name="offsets")
         nc.sync.dma_start(offsets[:], offs)
 
         mem_gate_sb = held.tile([P, 1], F32, name="mem_gate_sb")
-        nc.scalar.dma_start(mem_gate_sb[:], mem_gate)
+        nc.sync.dma_start(mem_gate_sb[:], mem_gate)
+        table_sb = held.tile([P, BLOCKS, P], BF16, name="table_sb")
+        nc.sync.dma_start(table_sb[:], table.rearrange("(b p) h -> p b h", p=P))
+
+        wm_sb = held.tile([P, P], BF16, name="wm_sb")
+        nc.scalar.dma_start(wm_sb[:], wm)
+        prev_sb = held.tile([P, N], BF16, name="prev_sb")
+        nc.scalar.dma_start(prev_sb[:], prev)
         bm_sb = held.tile([P, 1], F32, name="bm_sb")
         nc.scalar.dma_start(bm_sb[:], bm)
 

@@ -22,13 +22,12 @@ def tile_socialtnn_kernel(tc, table, prev, wm, bm, mem_gate, wq, bq, offs, out):
         tc.tile_pool(name="held", bufs=1) as held,
         tc.psum_pool(name="psum", bufs=1) as psum,
     ):
-        offsets = held.tile([P, N // 16], U16, name="offsets")
-        nc.sync.dma_start(offsets[:], offs)
-
         mem_gate_sb = held.tile([P, 1], F32, name="mem_gate_sb")
         nc.sync.dma_start(mem_gate_sb[:], mem_gate)
         table_sb = held.tile([P, BLOCKS, P], BF16, name="table_sb")
         nc.sync.dma_start(table_sb[:], table.rearrange("(b p) h -> p b h", p=P))
+        offsets = held.tile([P, N // 16], U16, name="offsets")
+        nc.sync.dma_start(offsets[:], offs)
 
         wm_sb = held.tile([P, P], BF16, name="wm_sb")
         nc.scalar.dma_start(wm_sb[:], wm)

@@ -22,6 +22,10 @@ def tile_socialtnn_kernel(tc, table, prev, wm, bm, mem_gate, wq, bq, offs, out):
         tc.tile_pool(name="held", bufs=1) as held,
         tc.psum_pool(name="psum", bufs=1) as psum,
     ):
+        wm_sb = held.tile([P, P], BF16, name="wm_sb")
+        nc.sync.dma_start(wm_sb[:], wm)
+        prev_sb = held.tile([P, N], BF16, name="prev_sb")
+        nc.sync.dma_start(prev_sb[:], prev)
         mem_gate_sb = held.tile([P, 1], F32, name="mem_gate_sb")
         nc.sync.dma_start(mem_gate_sb[:], mem_gate)
         table_sb = held.tile([P, BLOCKS, P], BF16, name="table_sb")
@@ -29,10 +33,6 @@ def tile_socialtnn_kernel(tc, table, prev, wm, bm, mem_gate, wq, bq, offs, out):
         offsets = held.tile([P, N // 16], U16, name="offsets")
         nc.sync.dma_start(offsets[:], offs)
 
-        wm_sb = held.tile([P, P], BF16, name="wm_sb")
-        nc.scalar.dma_start(wm_sb[:], wm)
-        prev_sb = held.tile([P, N], BF16, name="prev_sb")
-        nc.scalar.dma_start(prev_sb[:], prev)
         bm_sb = held.tile([P, 1], F32, name="bm_sb")
         nc.scalar.dma_start(bm_sb[:], bm)
 

@@ -49,6 +49,10 @@ def tile_socialtnn_kernel(tc, table, prev, wm, bm, mem_gate, wq, bq, offs, out):
         for i in range(WARM_MATMULS):
             nc.tensor.matmul(warm_ps[:], zeros[:, 0:P], zeros[:], start=True, stop=True)
 
+        table_warm = held.tile([P, 2], F32, name="table_warm")
+        nc.vector.memset(table_warm[:, 0:1], 0.0)
+        nc.scalar.activation(table_warm[:, 1:2], table_warm[:, 0:1], ACT.Sigmoid)
+
         one_minus_gate = held.tile([P, 1], F32, name="one_minus_gate")
         nc.scalar.activation(one_minus_gate[:], mem_gate_sb[:], ACT.Sigmoid, scale=-1.0)
         gate = held.tile([P, 1], F32, name="gate")

@@ -26,10 +26,10 @@ def tile_socialtnn_kernel(tc, table, prev, wm, bm, mem_gate, wq, bq, offs, out):
         nc.sync.dma_start(wm_sb[:], wm)
         prev_sb = held.tile([P, N], BF16, name="prev_sb")
         nc.sync.dma_start(prev_sb[:], prev)
-        mem_gate_sb = held.tile([P, 1], F32, name="mem_gate_sb")
-        nc.sync.dma_start(mem_gate_sb[:], mem_gate)
         table_sb = held.tile([P, BLOCKS, P], BF16, name="table_sb")
         nc.sync.dma_start(table_sb[:], table.rearrange("(b p) h -> p b h", p=P))
+        mem_gate_sb = held.tile([P, 1], F32, name="mem_gate_sb")
+        nc.sync.dma_start(mem_gate_sb[:], mem_gate)
         offsets = held.tile([P, N // 16], U16, name="offsets")
         nc.sync.dma_start(offsets[:], offs)
 

@@ -11,8 +11,6 @@ BF16, F32, U16 = mybir.dt.bfloat16, mybir.dt.float32, mybir.dt.uint16
 ACT = mybir.ActivationFunctionType
 ALU = mybir.AluOpType
 
-WARM_MATMULS = 4
-
 FLOPS = 3 * 2 * P * P * N
 
 
@@ -22,36 +20,25 @@ def tile_socialtnn_kernel(tc, table, prev, wm, bm, mem_gate, wq, bq, offs, out):
         tc.tile_pool(name="held", bufs=1) as held,
         tc.psum_pool(name="psum", bufs=1) as psum,
     ):
+        mem_gate_sb = held.tile([P, 1], F32, name="mem_gate_sb")
+        nc.scalar.dma_start(mem_gate_sb[:], mem_gate)
+        table_sb = held.tile([P, BLOCKS, P], BF16, name="table_sb")
+        nc.sync.dma_start(table_sb[:], table.rearrange("(b p) h -> p b h", p=P))
+        offsets = held.tile([P, N // 16], U16, name="offsets")
+        nc.sync.dma_start(offsets[:], offs)
         wm_sb = held.tile([P, P], BF16, name="wm_sb")
         nc.sync.dma_start(wm_sb[:], wm)
         prev_sb = held.tile([P, N], BF16, name="prev_sb")
         nc.sync.dma_start(prev_sb[:], prev)
-        table_sb = held.tile([P, BLOCKS, P], BF16, name="table_sb")
-        nc.sync.dma_start(table_sb[:], table.rearrange("(b p) h -> p b h", p=P))
-        mem_gate_sb = held.tile([P, 1], F32, name="mem_gate_sb")
-        nc.sync.dma_start(mem_gate_sb[:], mem_gate)
-        offsets = held.tile([P, N // 16], U16, name="offsets")
-        nc.sync.dma_start(offsets[:], offs)
-
         bm_sb = held.tile([P, 1], F32, name="bm_sb")
-        nc.scalar.dma_start(bm_sb[:], bm)
+        nc.sync.dma_start(bm_sb[:], bm)
+        wq_sb = held.tile([P, P], BF16, name="wq_sb")
+        nc.sync.dma_start(wq_sb[:], wq)
+        bq_sb = held.tile([P, 1], F32, name="bq_sb")
+        nc.sync.dma_start(bq_sb[:], bq)
 
         identity = held.tile([P, P], BF16, name="identity")
         make_identity(nc, identity[:])
-        wq_sb = held.tile([P, P], BF16, name="wq_sb")
-        nc.gpsimd.dma_start(wq_sb[:], wq)
-        bq_sb = held.tile([P, 1], F32, name="bq_sb")
-        nc.gpsimd.dma_start(bq_sb[:], bq)
-
-        zeros = held.tile([P, S], BF16, name="zeros")
-        nc.vector.memset(zeros[:], 0.0)
-        warm_ps = psum.tile([P, S], F32, name="warm_ps")
-        for i in range(WARM_MATMULS):
-            nc.tensor.matmul(warm_ps[:], zeros[:, 0:P], zeros[:], start=True, stop=True)
-
-        table_warm = held.tile([P, 2], F32, name="table_warm")
-        nc.vector.memset(table_warm[:, 0:1], 0.0)
-        nc.scalar.activation(table_warm[:, 1:2], table_warm[:, 0:1], ACT.Sigmoid)
 
         one_minus_gate = held.tile([P, 1], F32, name="one_minus_gate")
         nc.scalar.activation(one_minus_gate[:], mem_gate_sb[:], ACT.Sigmoid, scale=-1.0)

@@ -1,11 +1,11 @@
 import concourse.mybir as mybir
-from concourse.masks import make_identity
 
 P = 128
 S = 512
 N = 128
 BLOCKS = S // P
 HALF_BLOCKS = BLOCKS // 2
+BLOCK = 32
 
 BF16, F32, U16 = mybir.dt.bfloat16, mybir.dt.float32, mybir.dt.uint16
 ACT = mybir.ActivationFunctionType
@@ -20,25 +20,36 @@ def tile_socialtnn_kernel(tc, table, prev, wm, bm, mem_gate, wq, bq, offs, out):
         tc.tile_pool(name="held", bufs=1) as held,
         tc.psum_pool(name="psum", bufs=1) as psum,
     ):
-        mem_gate_sb = held.tile([P, 1], F32, name="mem_gate_sb")
-        nc.scalar.dma_start(mem_gate_sb[:], mem_gate)
         table_sb = held.tile([P, BLOCKS, P], BF16, name="table_sb")
         nc.sync.dma_start(table_sb[:], table.rearrange("(b p) h -> p b h", p=P))
+        mem_gate_sb = held.tile([P, 1], F32, name="mem_gate_sb")
+        nc.sync.dma_start(mem_gate_sb[:], mem_gate)
         offsets = held.tile([P, N // 16], U16, name="offsets")
         nc.sync.dma_start(offsets[:], offs)
-        wm_sb = held.tile([P, P], BF16, name="wm_sb")
-        nc.sync.dma_start(wm_sb[:], wm)
-        prev_sb = held.tile([P, N], BF16, name="prev_sb")
-        nc.sync.dma_start(prev_sb[:], prev)
-        bm_sb = held.tile([P, 1], F32, name="bm_sb")
-        nc.sync.dma_start(bm_sb[:], bm)
-        wq_sb = held.tile([P, P], BF16, name="wq_sb")
-        nc.sync.dma_start(wq_sb[:], wq)
         bq_sb = held.tile([P, 1], F32, name="bq_sb")
         nc.sync.dma_start(bq_sb[:], bq)
 
+        wm_sb = held.tile([P, P], BF16, name="wm_sb")
+        nc.scalar.dma_start(wm_sb[:], wm)
+        prev_sb = held.tile([P, N], BF16, name="prev_sb")
+        nc.scalar.dma_start(prev_sb[:], prev)
+        bm_sb = held.tile([P, 1], F32, name="bm_sb")
+        nc.scalar.dma_start(bm_sb[:], bm)
+
+        wq_sb = held.tile([P, P], BF16, name="wq_sb")
+        nc.scalar.dma_start(wq_sb[:], wq)
+
         identity = held.tile([P, P], BF16, name="identity")
-        make_identity(nc, identity[:])
+        nc.vector.memset(identity[:], 0.0)
+        ones = held.tile([P, BLOCK], F32, name="ones")
+        nc.vector.memset(ones[:], 1.0)
+        columns = held.tile([P, BLOCK], F32, name="columns", align_bytes=64)
+        nc.vector.tensor_tensor_scan(columns[:], ones[:], ones[:], 0.0, op0=ALU.mult, op1=ALU.add)
+        partitions = held.tile([P, BLOCK], F32, name="partitions", align_bytes=64)
+        nc.vector.transpose(partitions[:], columns[:])
+        for first in range(0, P, BLOCK):
+            block = slice(first, first + BLOCK)
+            nc.vector.tensor_tensor(identity[block, block], columns[block, :], partitions[block, :], op=ALU.is_equal)
 
         one_minus_gate = held.tile([P, 1], F32, name="one_minus_gate")
         nc.scalar.activation(one_minus_gate[:], mem_gate_sb[:], ACT.Sigmoid, scale=-1.0)
@@ -61,7 +72,7 @@ def tile_socialtnn_kernel(tc, table, prev, wm, bm, mem_gate, wq, bq, offs, out):
         tanh_sb = held.tile([P, N], F32, name="tanh_sb")
         nc.scalar.activation(tanh_sb[:], pre_ps[:], ACT.Tanh, bias=bm_sb[:, 0:1])
         memg_bf = held.tile([P, N], BF16, name="memg_bf")
-        nc.vector.tensor_scalar_mul(memg_bf[:], tanh_sb[:], gate[:, 0:1])
+        nc.scalar.activation(memg_bf[:], tanh_sb[:], ACT.Copy, scale=gate[:, 0:1])
 
         picked_ps = psum.tile([P, N], F32, name="picked_ps")
         nc.tensor.matmul(picked_ps[:], identity[:], ts[:].indirect(offsets[:]), start=True, stop=True)
@@ -69,11 +80,9 @@ def tile_socialtnn_kernel(tc, table, prev, wm, bm, mem_gate, wq, bq, offs, out):
         nc.tensor.matmul(q_ps[:], wq_sb[:], ts[:].indirect(offsets[:]), start=True, stop=False)
         nc.tensor.matmul(q_ps[:], wq_sb[:], memg_bf[:], start=False, stop=True)
 
-        h0_sb = held.tile([P, N], F32, name="h0_sb")
+        result = held.tile([P, 2, N], F32, name="result")
         nc.vector.scalar_tensor_tensor(
-            h0_sb[:], tanh_sb[:], gate[:, 0:1], picked_ps[:], op0=ALU.mult, op1=ALU.add
+            result[:, 0, :], tanh_sb[:], gate[:, 0:1], picked_ps[:], op0=ALU.mult, op1=ALU.add
         )
-        nc.sync.dma_start(out[0:P, :], h0_sb[:])
-        q_sb = held.tile([P, N], F32, name="q_sb")
-        nc.scalar.activation(q_sb[:], q_ps[:], ACT.Identity, bias=bq_sb[:, 0:1])
-        nc.scalar.dma_start(out[P : 2 * P, :], q_sb[:])
+        nc.scalar.activation(result[:, 1, :], q_ps[:], ACT.Identity, bias=bq_sb[:, 0:1])
+        nc.sync.dma_start(out.rearrange("(a p) n -> p a n", p=P), result[:])

@@ -28,6 +28,8 @@ def tile_socialtnn_kernel(tc, table, prev, wm, bm, mem_gate, wq, bq, offs, out):
         nc.sync.dma_start(offsets[:], offs)
         bq_sb = held.tile([P, 1], F32, name="bq_sb")
         nc.sync.dma_start(bq_sb[:], bq)
+        wq_sb = held.tile([P, P], BF16, name="wq_sb")
+        nc.sync.dma_start(wq_sb[:], wq)
 
         wm_sb = held.tile([P, P], BF16, name="wm_sb")
         nc.scalar.dma_start(wm_sb[:], wm)
@@ -35,9 +37,6 @@ def tile_socialtnn_kernel(tc, table, prev, wm, bm, mem_gate, wq, bq, offs, out):
         nc.scalar.dma_start(prev_sb[:], prev)
         bm_sb = held.tile([P, 1], F32, name="bm_sb")
         nc.scalar.dma_start(bm_sb[:], bm)
-
-        wq_sb = held.tile([P, P], BF16, name="wq_sb")
-        nc.scalar.dma_start(wq_sb[:], wq)
 
         identity = held.tile([P, P], BF16, name="identity")
         nc.vector.memset(identity[:], 0.0)
@@ -80,9 +79,11 @@ def tile_socialtnn_kernel(tc, table, prev, wm, bm, mem_gate, wq, bq, offs, out):
         nc.tensor.matmul(q_ps[:], wq_sb[:], ts[:].indirect(offsets[:]), start=True, stop=False)
         nc.tensor.matmul(q_ps[:], wq_sb[:], memg_bf[:], start=False, stop=True)
 
-        result = held.tile([P, 2, N], F32, name="result")
+        h0_sb = held.tile([P, N], F32, name="h0_sb")
         nc.vector.scalar_tensor_tensor(
-            result[:, 0, :], tanh_sb[:], gate[:, 0:1], picked_ps[:], op0=ALU.mult, op1=ALU.add
+            h0_sb[:], tanh_sb[:], gate[:, 0:1], picked_ps[:], op0=ALU.mult, op1=ALU.add
         )
-        nc.scalar.activation(result[:, 1, :], q_ps[:], ACT.Identity, bias=bq_sb[:, 0:1])
-        nc.sync.dma_start(out.rearrange("(a p) n -> p a n", p=P), result[:])
+        nc.sync.dma_start(out[0:P, :], h0_sb[:])
+        q_sb = held.tile([P, N], F32, name="q_sb")
+        nc.scalar.activation(q_sb[:], q_ps[:], ACT.Identity, bias=bq_sb[:, 0:1])
+        nc.scalar.dma_start(out[P : 2 * P, :], q_sb[:])

@@ -85,5 +85,5 @@ def tile_socialtnn_kernel(tc, table, prev, wm, bm, mem_gate, wq, bq, offs, out):
         )
         nc.sync.dma_start(out[0:P, :], h0_sb[:])
         q_sb = held.tile([P, N], F32, name="q_sb")
-        nc.scalar.activation(q_sb[:], q_ps[:], ACT.Identity, bias=bq_sb[:, 0:1])
-        nc.scalar.dma_start(out[P : 2 * P, :], q_sb[:])
+        nc.vector.tensor_scalar_add(q_sb[:], q_ps[:], bq_sb[:, 0:1])
+        nc.sync.dma_start(out[P : 2 * P, :], q_sb[:])

@@ -83,7 +83,7 @@ def tile_socialtnn_kernel(tc, table, prev, wm, bm, mem_gate, wq, bq, offs, out):
         nc.vector.scalar_tensor_tensor(
             h0_sb[:], tanh_sb[:], gate[:, 0:1], picked_ps[:], op0=ALU.mult, op1=ALU.add
         )
-        nc.sync.dma_start(out[0:P, :], h0_sb[:])
+        nc.scalar.dma_start(out[0:P, :], h0_sb[:])
         q_sb = held.tile([P, N], F32, name="q_sb")
         nc.vector.tensor_scalar_add(q_sb[:], q_ps[:], bq_sb[:, 0:1])
         nc.sync.dma_start(out[P : 2 * P, :], q_sb[:])

import concourse.mybir as mybir

P = 128
S = 512
N = 128
BLOCKS = S // P
HALF_BLOCKS = BLOCKS // 2
BLOCK = 32

BF16, F32, U16 = mybir.dt.bfloat16, mybir.dt.float32, mybir.dt.uint16
ACT = mybir.ActivationFunctionType
ALU = mybir.AluOpType

FLOPS = 3 * 2 * P * P * N


def tile_socialtnn_kernel(tc, table, prev, wm, bm, mem_gate, wq, bq, offs, out):
    nc = tc.nc
    with (
        tc.tile_pool(name="held", bufs=1) as held,
        tc.psum_pool(name="psum", bufs=1) as psum,
    ):
        table_sb = held.tile([P, BLOCKS, P], BF16, name="table_sb")
        nc.sync.dma_start(table_sb[:], table.rearrange("(b p) h -> p b h", p=P))
        mem_gate_sb = held.tile([P, 1], F32, name="mem_gate_sb")
        nc.sync.dma_start(mem_gate_sb[:], mem_gate)
        offsets = held.tile([P, N // 16], U16, name="offsets")
        nc.sync.dma_start(offsets[:], offs)
        bq_sb = held.tile([P, 1], F32, name="bq_sb")
        nc.sync.dma_start(bq_sb[:], bq)
        wq_sb = held.tile([P, P], BF16, name="wq_sb")
        nc.sync.dma_start(wq_sb[:], wq)

        wm_sb = held.tile([P, P], BF16, name="wm_sb")
        nc.scalar.dma_start(wm_sb[:], wm)
        prev_sb = held.tile([P, N], BF16, name="prev_sb")
        nc.scalar.dma_start(prev_sb[:], prev)
        bm_sb = held.tile([P, 1], F32, name="bm_sb")
        nc.scalar.dma_start(bm_sb[:], bm)

        identity = held.tile([P, P], BF16, name="identity")
        nc.vector.memset(identity[:], 0.0)
        ones = held.tile([P, BLOCK], F32, name="ones")
        nc.vector.memset(ones[:], 1.0)
        columns = held.tile([P, BLOCK], F32, name="columns", align_bytes=64)
        nc.vector.tensor_tensor_scan(columns[:], ones[:], ones[:], 0.0, op0=ALU.mult, op1=ALU.add)
        partitions = held.tile([P, BLOCK], F32, name="partitions", align_bytes=64)
        nc.vector.transpose(partitions[:], columns[:])
        for first in range(0, P, BLOCK):
            block = slice(first, first + BLOCK)
            nc.vector.tensor_tensor(identity[block, block], columns[block, :], partitions[block, :], op=ALU.is_equal)

        one_minus_gate = held.tile([P, 1], F32, name="one_minus_gate")
        nc.scalar.activation(one_minus_gate[:], mem_gate_sb[:], ACT.Sigmoid, scale=-1.0)
        gate = held.tile([P, 1], F32, name="gate")
        nc.scalar.activation(gate[:], mem_gate_sb[:], ACT.Sigmoid)

        ts = held.tile([P, S], BF16, name="ts")
        for half in range(2):
            table_t_ps = psum.tile([P, S // 2], BF16, name=f"table_t_ps{half}")
            for i in range(HALF_BLOCKS):
                nc.tensor.transpose(
                    table_t_ps[:, i * P : (i + 1) * P], table_sb[:, half * HALF_BLOCKS + i, :], identity[:]
                )
            nc.vector.tensor_scalar_mul(
                ts[:, half * (S // 2) : (half + 1) * (S // 2)], table_t_ps[:], one_minus_gate[:, 0:1]
            )

        pre_ps = psum.tile([P, N], F32, name="pre_ps")
        nc.tensor.matmul(pre_ps[:], wm_sb[:], prev_sb[:], start=True, stop=True)
        tanh_sb = held.tile([P, N], F32, name="tanh_sb")
        nc.scalar.activation(tanh_sb[:], pre_ps[:], ACT.Tanh, bias=bm_sb[:, 0:1])
        memg_bf = held.tile([P, N], BF16, name="memg_bf")
        nc.scalar.activation(memg_bf[:], tanh_sb[:], ACT.Copy, scale=gate[:, 0:1])

        picked_ps = psum.tile([P, N], F32, name="picked_ps")
        nc.tensor.matmul(picked_ps[:], identity[:], ts[:].indirect(offsets[:]), start=True, stop=True)
        q_ps = psum.tile([P, N], F32, name="q_ps")
        nc.tensor.matmul(q_ps[:], wq_sb[:], ts[:].indirect(offsets[:]), start=True, stop=False)
        nc.tensor.matmul(q_ps[:], wq_sb[:], memg_bf[:], start=False, stop=True)

        h0_sb = held.tile([P, N], F32, name="h0_sb")
        nc.vector.scalar_tensor_tensor(
            h0_sb[:], tanh_sb[:], gate[:, 0:1], picked_ps[:], op0=ALU.mult, op1=ALU.add
        )
        nc.scalar.dma_start(out[0:P, :], h0_sb[:])
        q_sb = held.tile([P, N], F32, name="q_sb")
        nc.vector.tensor_scalar_add(q_sb[:], q_ps[:], bq_sb[:, 0:1])
        nc.sync.dma_start(out[P : 2 * P, :], q_sb[:])
